import numpy as np
import ml_dtypes


def mxq(x, axis, fmt="e4m3"):
    dtype, down = {"e4m3": (ml_dtypes.float8_e4m3fn, 7), "e5m2": (ml_dtypes.float8_e5m2, 14)}[fmt]
    v = np.moveaxis(np.asarray(x, np.float32).astype(ml_dtypes.bfloat16).astype(np.float64), axis, -1)
    blocks = v.reshape(v.shape[:-1] + (-1, 32))
    amax = np.abs(blocks).max(-1, keepdims=True)
    byte = np.maximum(np.where(amax > 0, np.frexp(amax)[1] - 1 + 127, 0) - down, 1)
    scale = np.exp2(byte - 127.0)
    codes = (blocks / scale).astype(np.float32).astype(dtype).astype(np.float64)
    return np.moveaxis((codes * scale).reshape(v.shape), -1, axis)


BF16 = ml_dtypes.bfloat16


def bf(x):
    return np.asarray(x, np.float32).astype(BF16)


def f64(x):
    return np.asarray(x).astype(np.float64)


Q, K, D = 2048, 1024, 1024
EPS = 1e-6


def setup_inputs():
    p = np.random.standard_normal((K, D)) * 5.6 / np.sqrt(D)
    own = np.random.randint(0, K, Q)
    r = 1.0 + 2.0 * np.random.random_sample((Q, 1))
    q = p[own] + np.random.standard_normal((Q, D)) * r / np.sqrt(D)
    return {"class_prototypes": bf(p), "query_features": bf(q)}


def reference(class_prototypes, query_features):
    p = f64(class_prototypes)
    q = f64(query_features)
    d = q.shape[1]
    q_sq = np.sum(q * q, axis=1)
    p_sq = np.sum(p * p, axis=1)
    cross = mxq(q, 1, "e4m3") @ mxq(p, 1, "e4m3").T
    lin = 2.0 * EPS * (np.sum(q, axis=1)[:, None] - np.sum(p, axis=1)[None, :])
    sq = q_sq[:, None] + p_sq[None, :] - 2.0 * cross + lin + d * EPS * EPS
    dist = np.sqrt(np.maximum(sq, 0.0))
    post = np.exp(-dist)
    post = post / np.sum(post, axis=1, keepdims=True)
    c = np.max(post, axis=1)
    h = -np.sum(post * np.log(post), axis=1)
    return (post, c, h)

@@ -1,0 +1,251 @@
+from contextlib import ExitStack
+
+import concourse.mybir as mybir
+from concourse.masks import make_identity
+
+F32 = mybir.dt.float32
+BF16 = mybir.dt.bfloat16
+U32 = mybir.dt.uint32
+U8 = mybir.dt.uint8
+FP8X4 = mybir.dt.float8_e4m3fn_x4
+ACT = mybir.ActivationFunctionType
+ALU = mybir.AluOpType
+
+Q, K, D = 2048, 1024, 1024
+EPS = 1e-6
+P = 128
+QT = Q // P
+PT = K // P
+NH = 512
+FLOPS = 2 * Q * K * D
+
+AHEAD = 4
+PRE_STAT = 3
+EVAC_ON_VECTOR = (5, 6, 8, 10, 11, 13, 15,)
+NORM_ON_SCALAR = (1, 4, 7, 9, 12,)
+S_LAG = 2
+SQ_LAG = 1
+V2_LAG = 1
+Q_LAG = 1
+EX_LEAD = 1
+P_CHUNKS = ((0, 1), (1, 2), (2, 4), (4, 6), (6, 8))
+
+
+def tile_modalityspecificposterior_kernel(tc, class_prototypes, query_features, out_0, out_1, out_2):
+    nc = tc.nc
+    with ExitStack() as ctx:
+        keep = ctx.enter_context(tc.tile_pool(name="keep", bufs=1))
+        grp_pool = ctx.enter_context(tc.tile_pool(name="grp", bufs=3))
+        e_pool = ctx.enter_context(tc.tile_pool(name="epool", bufs=6))
+        post_pool = ctx.enter_context(tc.tile_pool(name="postpool", bufs=3))
+        ps_tr = ctx.enter_context(tc.psum_pool(name="pstr", bufs=4))
+        ps_acc = ctx.enter_context(tc.psum_pool(name="psacc", bufs=4))
+        ctx.enter_context(tc.manual_schedule())
+
+        p_view = class_prototypes.rearrange("(j p) d -> p j d", p=P)
+        q_view = query_features.rearrange("(p j) d -> p j d", j=QT)
+        o_view = out_0.rearrange("(p j) k -> p j k", j=QT)
+
+        p_nat = keep.tile([P, PT, D], BF16)
+        q_nat = keep.tile([P, QT, D], BF16)
+        for lo, hi in P_CHUNKS:
+            nc.sync.dma_start(out=p_nat[:, lo:hi, :], in_=p_view[:, lo:hi, :])
+        for c in range(8):
+            nc.sync.dma_start(out=q_nat[:, 2 * c:2 * c + 2, :], in_=q_view[:, 2 * c:2 * c + 2, :])
+
+        ident = keep.tile([P, P], F32)
+        make_identity(nc, ident[:])
+        eps_pos = keep.tile([P, 1], F32)
+        nc.vector.memset(eps_pos[:], EPS)
+        warm = keep.tile([P, 1], F32)
+        nc.scalar.activation(out=warm[:], in_=eps_pos[:], func=ACT.Sqrt)
+
+        p_grp = keep.tile([P, 2, K, 2], F32, align_bytes=64)
+        p_codes = keep.tile([P, 2, K], U32, align_bytes=64)
+        p_scales = keep.tile([P, 2, K], U8, align_bytes=64)
+        q_codes = keep.tile([P, QT, 2 * P], U32, align_bytes=64)
+        q_scales = keep.tile([P, QT, 2 * P], U8, align_bytes=64)
+        b_col = keep.tile([P, PT], F32)
+        b_row = keep.tile([P, K], F32)
+        a_all = keep.tile([P, QT], F32)
+        nega = keep.tile([P, QT], F32)
+        dist = keep.tile([P, QT, K + 8], F32)
+        s_all = keep.tile([P, QT], F32)
+        ed_all = keep.tile([P, QT], F32)
+        c_all = keep.tile([P, QT], F32)
+        h_all = keep.tile([P, QT], F32)
+        h_tmp = keep.tile([P, QT], F32)
+        ln_s = keep.tile([P, QT], F32)
+        junk32 = keep.tile([P, K], F32)
+        junk16 = keep.tile([P, D], BF16)
+
+        def transpose_words(src):
+            tr = ps_tr.tile([P, 4, P], F32, tag="tr")
+            words = src.bitcast(F32)
+            for w in range(4):
+                nc.tensor.transpose(tr[:, w, :], words[:, w * P:(w + 1) * P], ident[:])
+            return tr
+
+        tr_q = {}
+        grp_q = {}
+        acc_q = {}
+        e_tiles = {}
+
+        def q_transpose(j):
+            if j < QT:
+                tr_q[j] = transpose_words(q_nat[:, j, :])
+
+        def q_evacuate(j):
+            grp = grp_pool.tile([P, 2, P, 2], F32, align_bytes=64, tag="grp")
+            src = tr_q[j][:].rearrange("p (g u) i -> p g i u", g=2)
+            if j in EVAC_ON_VECTOR:
+                nc.vector.tensor_copy(out=grp[:], in_=src)
+            else:
+                nc.scalar.copy(out=grp[:], in_=src)
+            grp_q[j] = grp
+
+        def q_stat(j):
+            if j < QT:
+                nc.scalar.activation(out=junk16[:], in_=q_nat[:, j, :], func=ACT.Square,
+                                     bias=eps_pos[:, 0:1], scale=1.0, accum_out=a_all[:, j:j + 1])
+                nc.gpsimd.tensor_scalar(out=nega[:, j:j + 1], in0=a_all[:, j:j + 1], scalar1=-1.0,
+                                        scalar2=0.0, op0=ALU.mult, op1=ALU.add)
+
+        def q_quantise(j):
+            if j < QT:
+                nc.vector.quantize_mx(
+                    out=q_codes[:, j, :].bitcast(FP8X4), scales=q_scales[:, j, :],
+                    in_=grp_q[j][:].rearrange("p g i u -> p (g i u)").bitcast(BF16))
+
+        def q_cross(j):
+            if j < QT:
+                accs = []
+                for h in range(2):
+                    cols = slice(h * NH, (h + 1) * NH)
+                    acc = ps_acc.tile([P, NH], F32, tag="acc")
+                    for g in range(2):
+                        nc.tensor.matmul_mx(
+                            out=acc[:],
+                            lhsT=q_codes[:, j, g * P:(g + 1) * P].bitcast(FP8X4),
+                            lhsT_scale=q_scales[:, j, g * P:(g + 1) * P],
+                            rhs=p_codes[:, g, cols].bitcast(FP8X4),
+                            rhs_scale=p_scales[:, g, cols],
+                            start=(g == 0), stop=(g == 1))
+                    accs.append(acc)
+                acc_q[j] = accs
+
+        def q_add_b(j):
+            for h in range(2):
+                cols = slice(h * NH, (h + 1) * NH)
+                nc.vector.scalar_tensor_tensor(
+                    out=dist[:, j, cols], in0=acc_q[j][h][:], scalar=-2.0, in1=b_row[:, cols],
+                    op0=ALU.mult, op1=ALU.add)
+
+        def q_clamp_min(j):
+            nc.vector.tensor_scalar(
+                out=dist[:, j, 0:K], in0=dist[:, j, 0:K], scalar1=nega[:, j:j + 1], scalar2=None,
+                op0=ALU.max, op1=ALU.min, accum_out=dist[:, j, K:K + 1])
+
+        def q_sqrt(j):
+            nc.scalar.activation(out=dist[:, j, 0:K + 1], in_=dist[:, j, 0:K + 1], func=ACT.Sqrt,
+                                 bias=a_all[:, j:j + 1], scale=1.0)
+
+        def q_exp(j):
+            e = e_pool.tile([P, K], F32, tag="e")
+            e_tiles[j] = e
+            nc.scalar.activation(out=e[:], in_=dist[:, j, 0:K], func=ACT.Exp,
+                                 bias=dist[:, j, K:K + 1], scale=-1.0, accum_out=s_all[:, j:j + 1])
+
+        def q_recip(j):
+            nc.vector.reciprocal(out=c_all[:, j:j + 1], in_=s_all[:, j:j + 1])
+
+        def q_norm(j):
+            post = post_pool.tile([P, K], F32, tag="post")
+            if j in NORM_ON_SCALAR:
+                nc.scalar.activation(out=post[:], in_=e_tiles[j][:], func=ACT.Copy,
+                                     scale=c_all[:, j:j + 1])
+            else:
+                nc.vector.tensor_scalar(out=post[:], in0=e_tiles[j][:], scalar1=c_all[:, j:j + 1],
+                                        scalar2=None, op0=ALU.mult)
+            nc.sync.dma_start(out=o_view[:, j, :], in_=post[:])
+
+        def q_entropy_sum(j):
+            nc.vector.scalar_tensor_tensor(
+                out=junk32[:], in0=dist[:, j, 0:K], scalar=dist[:, j, K:K + 1], in1=e_tiles[j][:],
+                op0=ALU.subtract, op1=ALU.mult, accum_out=ed_all[:, j:j + 1])
+
+        for jj in range(PT):
+            tr = transpose_words(p_nat[:, jj, :])
+            nc.scalar.copy(out=p_grp[:, :, jj * P:(jj + 1) * P, :],
+                           in_=tr[:].rearrange("p (g u) i -> p g i u", g=2))
+            nc.vector.scalar_tensor_tensor(
+                out=junk32[:], in0=p_nat[:, jj, :], scalar=-2.0 * EPS, in1=p_nat[:, jj, :],
+                op0=ALU.add, op1=ALU.mult, accum_out=b_col[:, jj:jj + 1])
+        for h in range(2):
+            for g in range(2):
+                cols = slice(h * NH, (h + 1) * NH)
+                nc.vector.quantize_mx(
+                    out=p_codes[:, g, cols].bitcast(FP8X4),
+                    scales=p_scales[:, g, cols],
+                    in_=p_grp[:, g, cols, :].rearrange("p k u -> p (k u)").bitcast(BF16))
+        for j in range(AHEAD):
+            q_transpose(j)
+        acc_bs = []
+        for h in range(2):
+            acc_b = ps_acc.tile([P, NH], F32, tag="acc")
+            for s in range(4):
+                jj = 4 * h + s
+                nc.tensor.matmul(acc_b[:, s * P:(s + 1) * P],
+                                 lhsT=b_col[:, jj:jj + 1].to_broadcast([P, P]),
+                                 rhs=ident[:], start=True, stop=True)
+            acc_bs.append(acc_b)
+        for j in range(AHEAD):
+            q_evacuate(j)
+            if j < PRE_STAT:
+                q_stat(j)
+            if j >= Q_LAG:
+                q_quantise(j - Q_LAG)
+        for j in range(AHEAD, PRE_STAT):
+            q_stat(j)
+        for h in range(2):
+            nc.scalar.copy(out=b_row[:, h * NH:(h + 1) * NH], in_=acc_bs[h][:])
+        q_cross(0)
+
+        for j in range(QT + max(V2_LAG, SQ_LAG)):
+            q_cross(j + 1)
+            n = j + AHEAD
+            q_transpose(n)
+            if j < QT:
+                q_add_b(j)
+            if n < QT and n not in EVAC_ON_VECTOR:
+                q_evacuate(n)
+            q_stat(j + PRE_STAT)
+            if 0 <= j - V2_LAG < QT:
+                q_clamp_min(j - V2_LAG)
+            if n < QT and n in EVAC_ON_VECTOR:
+                q_evacuate(n)
+            q_quantise(n - Q_LAG)
+            if 0 <= j - SQ_LAG < QT:
+                q_sqrt(j - SQ_LAG)
+
+        for j in range(EX_LEAD):
+            q_exp(j)
+        q_recip(0)
+        for j in range(QT + S_LAG):
+            if j + EX_LEAD < QT:
+                q_exp(j + EX_LEAD)
+            elif j + EX_LEAD == QT:
+                nc.scalar.activation(out=ln_s[:], in_=s_all[:], func=ACT.Ln)
+            if j + 1 < QT:
+                q_recip(j + 1)
+            if j - S_LAG >= 0 and j - S_LAG in NORM_ON_SCALAR:
+                q_norm(j - S_LAG)
+            if j < QT:
+                if j not in NORM_ON_SCALAR:
+                    q_norm(j)
+                q_entropy_sum(j)
+
+        nc.sync.dma_start(out=out_1.rearrange("(p j) -> p j", j=QT), in_=c_all[:])
+        nc.vector.tensor_tensor(out=h_tmp[:], in0=ed_all[:], in1=c_all[:], op=ALU.mult)
+        nc.vector.tensor_tensor(out=h_all[:], in0=h_tmp[:], in1=ln_s[:], op=ALU.add)
+        nc.sync.dma_start(out=out_2.rearrange("(p j) -> p j", j=QT), in_=h_all[:])

@@ -21,10 +21,10 @@ FLOPS = 2 * Q * K * D
 
 AHEAD = 4
 PRE_STAT = 3
-EVAC_ON_VECTOR = (5, 6, 8, 10, 11, 13, 15,)
-NORM_ON_SCALAR = (1, 4, 7, 9, 12,)
+EVAC_ON_VECTOR = ()
+NORM_ON_SCALAR = (1, 3, 6, 8, 10, 12,)
 S_LAG = 2
-SQ_LAG = 1
+SQ_LAG = 2
 V2_LAG = 1
 Q_LAG = 1
 EX_LEAD = 1
@@ -37,7 +37,7 @@ def tile_modalityspecificposterior_kernel(tc, class_prototypes, query_features, 
         keep = ctx.enter_context(tc.tile_pool(name="keep", bufs=1))
         grp_pool = ctx.enter_context(tc.tile_pool(name="grp", bufs=3))
         e_pool = ctx.enter_context(tc.tile_pool(name="epool", bufs=6))
-        post_pool = ctx.enter_context(tc.tile_pool(name="postpool", bufs=3))
+        post_pool = ctx.enter_context(tc.tile_pool(name="postpool", bufs=5))
         ps_tr = ctx.enter_context(tc.psum_pool(name="pstr", bufs=4))
         ps_acc = ctx.enter_context(tc.psum_pool(name="psacc", bufs=4))
         ctx.enter_context(tc.manual_schedule())

@@ -23,11 +23,12 @@ AHEAD = 4
 PRE_STAT = 3
 EVAC_ON_VECTOR = ()
 NORM_ON_SCALAR = (1, 3, 6, 8, 10, 12,)
-S_LAG = 2
+S_LAG = 3
 SQ_LAG = 2
 V2_LAG = 1
 Q_LAG = 1
 EX_LEAD = 1
+P_STAT_ON_SCALAR = 7
 P_CHUNKS = ((0, 1), (1, 2), (2, 4), (4, 6), (6, 8))
 
 
@@ -78,6 +79,10 @@ def tile_modalityspecificposterior_kernel(tc, class_prototypes, query_features, 
         ln_s = keep.tile([P, QT], F32)
         junk32 = keep.tile([P, K], F32)
         junk16 = keep.tile([P, D], BF16)
+        eps_neg = keep.tile([P, 1], F32)
+        nc.vector.memset(eps_neg[:], -EPS)
+        b_raw = keep.tile([P, 1], F32)
+        b_fix = keep.tile([P, 1], F32)
 
         def transpose_words(src):
             tr = ps_tr.tile([P, 4, P], F32, tag="tr")
@@ -178,9 +183,14 @@ def tile_modalityspecificposterior_kernel(tc, class_prototypes, query_features, 
             tr = transpose_words(p_nat[:, jj, :])
             nc.scalar.copy(out=p_grp[:, :, jj * P:(jj + 1) * P, :],
                            in_=tr[:].rearrange("p (g u) i -> p g i u", g=2))
-            nc.vector.scalar_tensor_tensor(
-                out=junk32[:], in0=p_nat[:, jj, :], scalar=-2.0 * EPS, in1=p_nat[:, jj, :],
-                op0=ALU.add, op1=ALU.mult, accum_out=b_col[:, jj:jj + 1])
+            if jj != P_STAT_ON_SCALAR:
+                nc.vector.scalar_tensor_tensor(
+                    out=junk32[:], in0=p_nat[:, jj, :], scalar=-2.0 * EPS, in1=p_nat[:, jj, :],
+                    op0=ALU.add, op1=ALU.mult, accum_out=b_col[:, jj:jj + 1])
+        nc.scalar.activation(out=junk16[:], in_=p_nat[:, P_STAT_ON_SCALAR, :], func=ACT.Square,
+                             bias=eps_neg[:, 0:1], scale=1.0, accum_out=b_raw[:, 0:1])
+        nc.gpsimd.tensor_scalar(out=b_fix[:], in0=b_raw[:], scalar1=1.0, scalar2=-D * EPS * EPS,
+                                op0=ALU.mult, op1=ALU.add)
         for h in range(2):
             for g in range(2):
                 cols = slice(h * NH, (h + 1) * NH)
@@ -195,20 +205,22 @@ def tile_modalityspecificposterior_kernel(tc, class_prototypes, query_features, 
             acc_b = ps_acc.tile([P, NH], F32, tag="acc")
             for s in range(4):
                 jj = 4 * h + s
-                nc.tensor.matmul(acc_b[:, s * P:(s + 1) * P],
-                                 lhsT=b_col[:, jj:jj + 1].to_broadcast([P, P]),
+                col = b_fix[:, 0:1] if jj == P_STAT_ON_SCALAR else b_col[:, jj:jj + 1]
+                nc.tensor.matmul(acc_b[:, s * P:(s + 1) * P], lhsT=col.to_broadcast([P, P]),
                                  rhs=ident[:], start=True, stop=True)
             acc_bs.append(acc_b)
-        for j in range(AHEAD):
-            q_evacuate(j)
-            if j < PRE_STAT:
-                q_stat(j)
-            if j >= Q_LAG:
-                q_quantise(j - Q_LAG)
-        for j in range(AHEAD, PRE_STAT):
-            q_stat(j)
+        q_evacuate(0)
+        q_evacuate(1)
+        q_stat(0)
+        q_quantise(0)
+        q_quantise(1)
         for h in range(2):
             nc.scalar.copy(out=b_row[:, h * NH:(h + 1) * NH], in_=acc_bs[h][:])
+        q_evacuate(2)
+        q_stat(1)
+        q_quantise(2)
+        q_evacuate(3)
+        q_stat(2)
         q_cross(0)
 
         for j in range(QT + max(V2_LAG, SQ_LAG)):
@@ -228,22 +240,18 @@ def tile_modalityspecificposterior_kernel(tc, class_prototypes, query_features, 
             if 0 <= j - SQ_LAG < QT:
                 q_sqrt(j - SQ_LAG)
 
-        for j in range(EX_LEAD):
-            q_exp(j)
-        q_recip(0)
         for j in range(QT + S_LAG):
-            if j + EX_LEAD < QT:
-                q_exp(j + EX_LEAD)
-            elif j + EX_LEAD == QT:
+            if j < QT:
+                q_exp(j)
+            elif j == QT:
                 nc.scalar.activation(out=ln_s[:], in_=s_all[:], func=ACT.Ln)
-            if j + 1 < QT:
-                q_recip(j + 1)
             if j - S_LAG >= 0 and j - S_LAG in NORM_ON_SCALAR:
                 q_norm(j - S_LAG)
             if j < QT:
+                q_recip(j)
+                q_entropy_sum(j)
                 if j not in NORM_ON_SCALAR:
                     q_norm(j)
-                q_entropy_sum(j)
 
         nc.sync.dma_start(out=out_1.rearrange("(p j) -> p j", j=QT), in_=c_all[:])
         nc.vector.tensor_tensor(out=h_tmp[:], in0=ed_all[:], in1=c_all[:], op=ALU.mult)

@@ -21,15 +21,13 @@ FLOPS = 2 * Q * K * D
 
 AHEAD = 4
 PRE_STAT = 3
-EVAC_ON_VECTOR = ()
 NORM_ON_SCALAR = (1, 3, 6, 8, 10, 12,)
 S_LAG = 3
 SQ_LAG = 2
-V2_LAG = 1
-Q_LAG = 1
-EX_LEAD = 1
 P_STAT_ON_SCALAR = 7
 P_CHUNKS = ((0, 1), (1, 2), (2, 4), (4, 6), (6, 8))
+SPLIT = True
+LAST = QT - 1
 
 
 def tile_modalityspecificposterior_kernel(tc, class_prototypes, query_features, out_0, out_1, out_2):
@@ -58,6 +56,10 @@ def tile_modalityspecificposterior_kernel(tc, class_prototypes, query_features, 
         make_identity(nc, ident[:])
         eps_pos = keep.tile([P, 1], F32)
         nc.vector.memset(eps_pos[:], EPS)
+        eps_neg = keep.tile([P, 1], F32)
+        nc.vector.memset(eps_neg[:], -EPS)
+        b_shift = keep.tile([P, 1], F32)
+        nc.vector.memset(b_shift[:], -D * EPS * EPS)
         warm = keep.tile([P, 1], F32)
         nc.scalar.activation(out=warm[:], in_=eps_pos[:], func=ACT.Sqrt)
 
@@ -67,22 +69,22 @@ def tile_modalityspecificposterior_kernel(tc, class_prototypes, query_features, 
         q_codes = keep.tile([P, QT, 2 * P], U32, align_bytes=64)
         q_scales = keep.tile([P, QT, 2 * P], U8, align_bytes=64)
         b_col = keep.tile([P, PT], F32)
+        b_raw = keep.tile([P, 1], F32)
+        b_fix = keep.tile([P, 1], F32)
         b_row = keep.tile([P, K], F32)
         a_all = keep.tile([P, QT], F32)
-        nega = keep.tile([P, QT], F32)
         dist = keep.tile([P, QT, K + 8], F32)
         s_all = keep.tile([P, QT], F32)
+        s_half = keep.tile([P, 2], F32)
+        s_first = keep.tile([P, 1], F32)
         ed_all = keep.tile([P, QT], F32)
+        ed_half = keep.tile([P, 2], F32)
         c_all = keep.tile([P, QT], F32)
         h_all = keep.tile([P, QT], F32)
         h_tmp = keep.tile([P, QT], F32)
-        ln_s = keep.tile([P, QT], F32)
+        ln_c = keep.tile([P, QT], F32)
         junk32 = keep.tile([P, K], F32)
         junk16 = keep.tile([P, D], BF16)
-        eps_neg = keep.tile([P, 1], F32)
-        nc.vector.memset(eps_neg[:], -EPS)
-        b_raw = keep.tile([P, 1], F32)
-        b_fix = keep.tile([P, 1], F32)
 
         def transpose_words(src):
             tr = ps_tr.tile([P, 4, P], F32, tag="tr")
@@ -101,20 +103,15 @@ def tile_modalityspecificposterior_kernel(tc, class_prototypes, query_features, 
                 tr_q[j] = transpose_words(q_nat[:, j, :])
 
         def q_evacuate(j):
-            grp = grp_pool.tile([P, 2, P, 2], F32, align_bytes=64, tag="grp")
-            src = tr_q[j][:].rearrange("p (g u) i -> p g i u", g=2)
-            if j in EVAC_ON_VECTOR:
-                nc.vector.tensor_copy(out=grp[:], in_=src)
-            else:
-                nc.scalar.copy(out=grp[:], in_=src)
-            grp_q[j] = grp
+            if j < QT:
+                grp = grp_pool.tile([P, 2, P, 2], F32, align_bytes=64, tag="grp")
+                nc.scalar.copy(out=grp[:], in_=tr_q[j][:].rearrange("p (g u) i -> p g i u", g=2))
+                grp_q[j] = grp
 
         def q_stat(j):
             if j < QT:
                 nc.scalar.activation(out=junk16[:], in_=q_nat[:, j, :], func=ACT.Square,
                                      bias=eps_pos[:, 0:1], scale=1.0, accum_out=a_all[:, j:j + 1])
-                nc.gpsimd.tensor_scalar(out=nega[:, j:j + 1], in0=a_all[:, j:j + 1], scalar1=-1.0,
-                                        scalar2=0.0, op0=ALU.mult, op1=ALU.add)
 
         def q_quantise(j):
             if j < QT:
@@ -139,30 +136,25 @@ def tile_modalityspecificposterior_kernel(tc, class_prototypes, query_features, 
                     accs.append(acc)
                 acc_q[j] = accs
 
-        def q_add_b(j):
+        def q_sub_b(j):
             for h in range(2):
                 cols = slice(h * NH, (h + 1) * NH)
                 nc.vector.scalar_tensor_tensor(
-                    out=dist[:, j, cols], in0=acc_q[j][h][:], scalar=-2.0, in1=b_row[:, cols],
-                    op0=ALU.mult, op1=ALU.add)
+                    out=dist[:, j, cols], in0=acc_q[j][h][:], scalar=2.0, in1=b_row[:, cols],
+                    op0=ALU.mult, op1=ALU.subtract)
 
-        def q_clamp_min(j):
+        def q_clamp_max(j, lo, hi, slot):
             nc.vector.tensor_scalar(
-                out=dist[:, j, 0:K], in0=dist[:, j, 0:K], scalar1=nega[:, j:j + 1], scalar2=None,
-                op0=ALU.max, op1=ALU.min, accum_out=dist[:, j, K:K + 1])
+                out=dist[:, j, lo:hi], in0=dist[:, j, lo:hi], scalar1=a_all[:, j:j + 1], scalar2=None,
+                op0=ALU.min, op1=ALU.max, accum_out=dist[:, j, K + slot:K + slot + 1])
 
-        def q_sqrt(j):
-            nc.scalar.activation(out=dist[:, j, 0:K + 1], in_=dist[:, j, 0:K + 1], func=ACT.Sqrt,
-                                 bias=a_all[:, j:j + 1], scale=1.0)
+        def q_sqrt(j, lo, hi):
+            nc.scalar.activation(out=dist[:, j, lo:hi], in_=dist[:, j, lo:hi], func=ACT.Sqrt,
+                                 bias=a_all[:, j:j + 1], scale=-1.0)
 
-        def q_exp(j):
-            e = e_pool.tile([P, K], F32, tag="e")
-            e_tiles[j] = e
-            nc.scalar.activation(out=e[:], in_=dist[:, j, 0:K], func=ACT.Exp,
-                                 bias=dist[:, j, K:K + 1], scale=-1.0, accum_out=s_all[:, j:j + 1])
-
-        def q_recip(j):
-            nc.vector.reciprocal(out=c_all[:, j:j + 1], in_=s_all[:, j:j + 1])
+        def q_exp(j, lo, hi, acc_out):
+            nc.scalar.activation(out=e_tiles[j][:, lo:hi], in_=dist[:, j, lo:hi], func=ACT.Exp,
+                                 bias=dist[:, j, K:K + 1], scale=-1.0, accum_out=acc_out)
 
         def q_norm(j):
             post = post_pool.tile([P, K], F32, tag="post")
@@ -174,10 +166,10 @@ def tile_modalityspecificposterior_kernel(tc, class_prototypes, query_features, 
                                         scalar2=None, op0=ALU.mult)
             nc.sync.dma_start(out=o_view[:, j, :], in_=post[:])
 
-        def q_entropy_sum(j):
+        def q_entropy_sum(j, lo, hi, acc_out):
             nc.vector.scalar_tensor_tensor(
-                out=junk32[:], in0=dist[:, j, 0:K], scalar=dist[:, j, K:K + 1], in1=e_tiles[j][:],
-                op0=ALU.subtract, op1=ALU.mult, accum_out=ed_all[:, j:j + 1])
+                out=junk32[:, lo:hi], in0=dist[:, j, lo:hi], scalar=dist[:, j, K:K + 1],
+                in1=e_tiles[j][:, lo:hi], op0=ALU.subtract, op1=ALU.mult, accum_out=acc_out)
 
         for jj in range(PT):
             tr = transpose_words(p_nat[:, jj, :])
@@ -189,8 +181,10 @@ def tile_modalityspecificposterior_kernel(tc, class_prototypes, query_features, 
                     op0=ALU.add, op1=ALU.mult, accum_out=b_col[:, jj:jj + 1])
         nc.scalar.activation(out=junk16[:], in_=p_nat[:, P_STAT_ON_SCALAR, :], func=ACT.Square,
                              bias=eps_neg[:, 0:1], scale=1.0, accum_out=b_raw[:, 0:1])
-        nc.gpsimd.tensor_scalar(out=b_fix[:], in0=b_raw[:], scalar1=1.0, scalar2=-D * EPS * EPS,
-                                op0=ALU.mult, op1=ALU.add)
+        q_transpose(0)
+        q_evacuate(0)
+        nc.scalar.activation(out=b_fix[:], in_=b_raw[:], func=ACT.Identity, bias=b_shift[:, 0:1],
+                             scale=1.0)
         for h in range(2):
             for g in range(2):
                 cols = slice(h * NH, (h + 1) * NH)
@@ -198,7 +192,7 @@ def tile_modalityspecificposterior_kernel(tc, class_prototypes, query_features, 
                     out=p_codes[:, g, cols].bitcast(FP8X4),
                     scales=p_scales[:, g, cols],
                     in_=p_grp[:, g, cols, :].rearrange("p k u -> p (k u)").bitcast(BF16))
-        for j in range(AHEAD):
+        for j in range(1, AHEAD):
             q_transpose(j)
         acc_bs = []
         for h in range(2):
@@ -209,7 +203,6 @@ def tile_modalityspecificposterior_kernel(tc, class_prototypes, query_features, 
                 nc.tensor.matmul(acc_b[:, s * P:(s + 1) * P], lhsT=col.to_broadcast([P, P]),
                                  rhs=ident[:], start=True, stop=True)
             acc_bs.append(acc_b)
-        q_evacuate(0)
         q_evacuate(1)
         q_stat(0)
         q_quantise(0)
@@ -223,37 +216,61 @@ def tile_modalityspecificposterior_kernel(tc, class_prototypes, query_features, 
         q_stat(2)
         q_cross(0)
 
-        for j in range(QT + max(V2_LAG, SQ_LAG)):
+        for j in range(QT + SQ_LAG):
             q_cross(j + 1)
-            n = j + AHEAD
-            q_transpose(n)
+            q_transpose(j + AHEAD)
             if j < QT:
-                q_add_b(j)
-            if n < QT and n not in EVAC_ON_VECTOR:
-                q_evacuate(n)
+                q_sub_b(j)
+            q_evacuate(j + AHEAD)
             q_stat(j + PRE_STAT)
-            if 0 <= j - V2_LAG < QT:
-                q_clamp_min(j - V2_LAG)
-            if n < QT and n in EVAC_ON_VECTOR:
-                q_evacuate(n)
-            q_quantise(n - Q_LAG)
-            if 0 <= j - SQ_LAG < QT:
-                q_sqrt(j - SQ_LAG)
+            if 1 <= j <= QT:
+                if SPLIT and j - 1 == LAST:
+                    q_clamp_max(LAST, 0, NH, 0)
+                    q_clamp_max(LAST, NH, K, 1)
+                else:
+                    q_clamp_max(j - 1, 0, K, 0)
+            q_quantise(j + AHEAD - 1)
+            if j >= SQ_LAG:
+                if SPLIT and j - SQ_LAG == LAST:
+                    q_sqrt(LAST, 0, NH)
+                    q_sqrt(LAST, NH, K + 2)
+                    nc.vector.tensor_tensor(out=dist[:, LAST, K:K + 1], in0=dist[:, LAST, K:K + 1],
+                                            in1=dist[:, LAST, K + 1:K + 2], op=ALU.min)
+                else:
+                    q_sqrt(j - SQ_LAG, 0, K + 1)
 
         for j in range(QT + S_LAG):
             if j < QT:
-                q_exp(j)
-            elif j == QT:
-                nc.scalar.activation(out=ln_s[:], in_=s_all[:], func=ACT.Ln)
+                e_tiles[j] = e_pool.tile([P, K], F32, tag="e", name="e")
+                if SPLIT and j == 0:
+                    q_exp(0, 0, NH, s_half[:, 0:1])
+                    q_exp(0, NH, K, s_half[:, 1:2])
+                else:
+                    q_exp(j, 0, K, s_all[:, j:j + 1])
             if j - S_LAG >= 0 and j - S_LAG in NORM_ON_SCALAR:
                 q_norm(j - S_LAG)
             if j < QT:
-                q_recip(j)
-                q_entropy_sum(j)
-                if j not in NORM_ON_SCALAR:
+                if SPLIT and j == 0:
+                    q_entropy_sum(0, 0, NH, ed_half[:, 0:1])
+                    q_entropy_sum(0, NH, K, ed_half[:, 1:2])
+                    nc.vector.tensor_tensor(out=s_first[:], in0=s_half[:, 0:1], in1=s_half[:, 1:2],
+                                            op=ALU.add)
+                    nc.vector.tensor_tensor(out=ed_all[:, 0:1], in0=ed_half[:, 0:1],
+                                            in1=ed_half[:, 1:2], op=ALU.add)
+                    nc.vector.reciprocal(out=c_all[:, 0:1], in_=s_first[:])
+                    q_norm(0)
+                elif j == LAST:
+                    nc.vector.reciprocal(out=c_all[:, j:j + 1], in_=s_all[:, j:j + 1])
+                    nc.scalar.activation(out=ln_c[:], in_=c_all[:], func=ACT.Ln)
                     q_norm(j)
+                    q_entropy_sum(j, 0, K, ed_all[:, j:j + 1])
+                else:
+                    nc.vector.reciprocal(out=c_all[:, j:j + 1], in_=s_all[:, j:j + 1])
+                    q_entropy_sum(j, 0, K, ed_all[:, j:j + 1])
+                    if j not in NORM_ON_SCALAR:
+                        q_norm(j)
 
         nc.sync.dma_start(out=out_1.rearrange("(p j) -> p j", j=QT), in_=c_all[:])
         nc.vector.tensor_tensor(out=h_tmp[:], in0=ed_all[:], in1=c_all[:], op=ALU.mult)
-        nc.vector.tensor_tensor(out=h_all[:], in0=h_tmp[:], in1=ln_s[:], op=ALU.add)
+        nc.vector.tensor_tensor(out=h_all[:], in0=h_tmp[:], in1=ln_c[:], op=ALU.subtract)
         nc.sync.dma_start(out=out_2.rearrange("(p j) -> p j", j=QT), in_=h_all[:])

@@ -21,7 +21,7 @@ FLOPS = 2 * Q * K * D
 
 AHEAD = 4
 PRE_STAT = 3
-NORM_ON_SCALAR = (1, 3, 6, 8, 10, 12,)
+NORM_ON_SCALAR = (1, 3, 5, 7, 9, 11, 13,)
 S_LAG = 3
 SQ_LAG = 2
 P_STAT_ON_SCALAR = 7

from contextlib import ExitStack

import concourse.mybir as mybir
from concourse.masks import make_identity

F32 = mybir.dt.float32
BF16 = mybir.dt.bfloat16
U32 = mybir.dt.uint32
U8 = mybir.dt.uint8
FP8X4 = mybir.dt.float8_e4m3fn_x4
ACT = mybir.ActivationFunctionType
ALU = mybir.AluOpType

Q, K, D = 2048, 1024, 1024
EPS = 1e-6
P = 128
QT = Q // P
PT = K // P
NH = 512
FLOPS = 2 * Q * K * D

AHEAD = 4
PRE_STAT = 3
NORM_ON_SCALAR = (1, 3, 5, 7, 9, 11, 13,)
S_LAG = 3
SQ_LAG = 2
P_STAT_ON_SCALAR = 7
P_CHUNKS = ((0, 1), (1, 2), (2, 4), (4, 6), (6, 8))
SPLIT = True
LAST = QT - 1


def tile_modalityspecificposterior_kernel(tc, class_prototypes, query_features, out_0, out_1, out_2):
    nc = tc.nc
    with ExitStack() as ctx:
        keep = ctx.enter_context(tc.tile_pool(name="keep", bufs=1))
        grp_pool = ctx.enter_context(tc.tile_pool(name="grp", bufs=3))
        e_pool = ctx.enter_context(tc.tile_pool(name="epool", bufs=6))
        post_pool = ctx.enter_context(tc.tile_pool(name="postpool", bufs=5))
        ps_tr = ctx.enter_context(tc.psum_pool(name="pstr", bufs=4))
        ps_acc = ctx.enter_context(tc.psum_pool(name="psacc", bufs=4))
        ctx.enter_context(tc.manual_schedule())

        p_view = class_prototypes.rearrange("(j p) d -> p j d", p=P)
        q_view = query_features.rearrange("(p j) d -> p j d", j=QT)
        o_view = out_0.rearrange("(p j) k -> p j k", j=QT)

        p_nat = keep.tile([P, PT, D], BF16)
        q_nat = keep.tile([P, QT, D], BF16)
        for lo, hi in P_CHUNKS:
            nc.sync.dma_start(out=p_nat[:, lo:hi, :], in_=p_view[:, lo:hi, :])
        for c in range(8):
            nc.sync.dma_start(out=q_nat[:, 2 * c:2 * c + 2, :], in_=q_view[:, 2 * c:2 * c + 2, :])

        ident = keep.tile([P, P], F32)
        make_identity(nc, ident[:])
        eps_pos = keep.tile([P, 1], F32)
        nc.vector.memset(eps_pos[:], EPS)
        eps_neg = keep.tile([P, 1], F32)
        nc.vector.memset(eps_neg[:], -EPS)
        b_shift = keep.tile([P, 1], F32)
        nc.vector.memset(b_shift[:], -D * EPS * EPS)
        warm = keep.tile([P, 1], F32)
        nc.scalar.activation(out=warm[:], in_=eps_pos[:], func=ACT.Sqrt)

        p_grp = keep.tile([P, 2, K, 2], F32, align_bytes=64)
        p_codes = keep.tile([P, 2, K], U32, align_bytes=64)
        p_scales = keep.tile([P, 2, K], U8, align_bytes=64)
        q_codes = keep.tile([P, QT, 2 * P], U32, align_bytes=64)
        q_scales = keep.tile([P, QT, 2 * P], U8, align_bytes=64)
        b_col = keep.tile([P, PT], F32)
        b_raw = keep.tile([P, 1], F32)
        b_fix = keep.tile([P, 1], F32)
        b_row = keep.tile([P, K], F32)
        a_all = keep.tile([P, QT], F32)
        dist = keep.tile([P, QT, K + 8], F32)
        s_all = keep.tile([P, QT], F32)
        s_half = keep.tile([P, 2], F32)
        s_first = keep.tile([P, 1], F32)
        ed_all = keep.tile([P, QT], F32)
        ed_half = keep.tile([P, 2], F32)
        c_all = keep.tile([P, QT], F32)
        h_all = keep.tile([P, QT], F32)
        h_tmp = keep.tile([P, QT], F32)
        ln_c = keep.tile([P, QT], F32)
        junk32 = keep.tile([P, K], F32)
        junk16 = keep.tile([P, D], BF16)

        def transpose_words(src):
            tr = ps_tr.tile([P, 4, P], F32, tag="tr")
            words = src.bitcast(F32)
            for w in range(4):
                nc.tensor.transpose(tr[:, w, :], words[:, w * P:(w + 1) * P], ident[:])
            return tr

        tr_q = {}
        grp_q = {}
        acc_q = {}
        e_tiles = {}

        def q_transpose(j):
            if j < QT:
                tr_q[j] = transpose_words(q_nat[:, j, :])

        def q_evacuate(j):
            if j < QT:
                grp = grp_pool.tile([P, 2, P, 2], F32, align_bytes=64, tag="grp")
                nc.scalar.copy(out=grp[:], in_=tr_q[j][:].rearrange("p (g u) i -> p g i u", g=2))
                grp_q[j] = grp

        def q_stat(j):
            if j < QT:
                nc.scalar.activation(out=junk16[:], in_=q_nat[:, j, :], func=ACT.Square,
                                     bias=eps_pos[:, 0:1], scale=1.0, accum_out=a_all[:, j:j + 1])

        def q_quantise(j):
            if j < QT:
                nc.vector.quantize_mx(
                    out=q_codes[:, j, :].bitcast(FP8X4), scales=q_scales[:, j, :],
                    in_=grp_q[j][:].rearrange("p g i u -> p (g i u)").bitcast(BF16))

        def q_cross(j):
            if j < QT:
                accs = []
                for h in range(2):
                    cols = slice(h * NH, (h + 1) * NH)
                    acc = ps_acc.tile([P, NH], F32, tag="acc")
                    for g in range(2):
                        nc.tensor.matmul_mx(
                            out=acc[:],
                            lhsT=q_codes[:, j, g * P:(g + 1) * P].bitcast(FP8X4),
                            lhsT_scale=q_scales[:, j, g * P:(g + 1) * P],
                            rhs=p_codes[:, g, cols].bitcast(FP8X4),
                            rhs_scale=p_scales[:, g, cols],
                            start=(g == 0), stop=(g == 1))
                    accs.append(acc)
                acc_q[j] = accs

        def q_sub_b(j):
            for h in range(2):
                cols = slice(h * NH, (h + 1) * NH)
                nc.vector.scalar_tensor_tensor(
                    out=dist[:, j, cols], in0=acc_q[j][h][:], scalar=2.0, in1=b_row[:, cols],
                    op0=ALU.mult, op1=ALU.subtract)

        def q_clamp_max(j, lo, hi, slot):
            nc.vector.tensor_scalar(
                out=dist[:, j, lo:hi], in0=dist[:, j, lo:hi], scalar1=a_all[:, j:j + 1], scalar2=None,
                op0=ALU.min, op1=ALU.max, accum_out=dist[:, j, K + slot:K + slot + 1])

        def q_sqrt(j, lo, hi):
            nc.scalar.activation(out=dist[:, j, lo:hi], in_=dist[:, j, lo:hi], func=ACT.Sqrt,
                                 bias=a_all[:, j:j + 1], scale=-1.0)

        def q_exp(j, lo, hi, acc_out):
            nc.scalar.activation(out=e_tiles[j][:, lo:hi], in_=dist[:, j, lo:hi], func=ACT.Exp,
                                 bias=dist[:, j, K:K + 1], scale=-1.0, accum_out=acc_out)

        def q_norm(j):
            post = post_pool.tile([P, K], F32, tag="post")
            if j in NORM_ON_SCALAR:
                nc.scalar.activation(out=post[:], in_=e_tiles[j][:], func=ACT.Copy,
                                     scale=c_all[:, j:j + 1])
            else:
                nc.vector.tensor_scalar(out=post[:], in0=e_tiles[j][:], scalar1=c_all[:, j:j + 1],
                                        scalar2=None, op0=ALU.mult)
            nc.sync.dma_start(out=o_view[:, j, :], in_=post[:])

        def q_entropy_sum(j, lo, hi, acc_out):
            nc.vector.scalar_tensor_tensor(
                out=junk32[:, lo:hi], in0=dist[:, j, lo:hi], scalar=dist[:, j, K:K + 1],
                in1=e_tiles[j][:, lo:hi], op0=ALU.subtract, op1=ALU.mult, accum_out=acc_out)

        for jj in range(PT):
            tr = transpose_words(p_nat[:, jj, :])
            nc.scalar.copy(out=p_grp[:, :, jj * P:(jj + 1) * P, :],
                           in_=tr[:].rearrange("p (g u) i -> p g i u", g=2))
            if jj != P_STAT_ON_SCALAR:
                nc.vector.scalar_tensor_tensor(
                    out=junk32[:], in0=p_nat[:, jj, :], scalar=-2.0 * EPS, in1=p_nat[:, jj, :],
                    op0=ALU.add, op1=ALU.mult, accum_out=b_col[:, jj:jj + 1])
        nc.scalar.activation(out=junk16[:], in_=p_nat[:, P_STAT_ON_SCALAR, :], func=ACT.Square,
                             bias=eps_neg[:, 0:1], scale=1.0, accum_out=b_raw[:, 0:1])
        q_transpose(0)
        q_evacuate(0)
        nc.scalar.activation(out=b_fix[:], in_=b_raw[:], func=ACT.Identity, bias=b_shift[:, 0:1],
                             scale=1.0)
        for h in range(2):
            for g in range(2):
                cols = slice(h * NH, (h + 1) * NH)
                nc.vector.quantize_mx(
                    out=p_codes[:, g, cols].bitcast(FP8X4),
                    scales=p_scales[:, g, cols],
                    in_=p_grp[:, g, cols, :].rearrange("p k u -> p (k u)").bitcast(BF16))
        for j in range(1, AHEAD):
            q_transpose(j)
        acc_bs = []
        for h in range(2):
            acc_b = ps_acc.tile([P, NH], F32, tag="acc")
            for s in range(4):
                jj = 4 * h + s
                col = b_fix[:, 0:1] if jj == P_STAT_ON_SCALAR else b_col[:, jj:jj + 1]
                nc.tensor.matmul(acc_b[:, s * P:(s + 1) * P], lhsT=col.to_broadcast([P, P]),
                                 rhs=ident[:], start=True, stop=True)
            acc_bs.append(acc_b)
        q_evacuate(1)
        q_stat(0)
        q_quantise(0)
        q_quantise(1)
        for h in range(2):
            nc.scalar.copy(out=b_row[:, h * NH:(h + 1) * NH], in_=acc_bs[h][:])
        q_evacuate(2)
        q_stat(1)
        q_quantise(2)
        q_evacuate(3)
        q_stat(2)
        q_cross(0)

        for j in range(QT + SQ_LAG):
            q_cross(j + 1)
            q_transpose(j + AHEAD)
            if j < QT:
                q_sub_b(j)
            q_evacuate(j + AHEAD)
            q_stat(j + PRE_STAT)
            if 1 <= j <= QT:
                if SPLIT and j - 1 == LAST:
                    q_clamp_max(LAST, 0, NH, 0)
                    q_clamp_max(LAST, NH, K, 1)
                else:
                    q_clamp_max(j - 1, 0, K, 0)
            q_quantise(j + AHEAD - 1)
            if j >= SQ_LAG:
                if SPLIT and j - SQ_LAG == LAST:
                    q_sqrt(LAST, 0, NH)
                    q_sqrt(LAST, NH, K + 2)
                    nc.vector.tensor_tensor(out=dist[:, LAST, K:K + 1], in0=dist[:, LAST, K:K + 1],
                                            in1=dist[:, LAST, K + 1:K + 2], op=ALU.min)
                else:
                    q_sqrt(j - SQ_LAG, 0, K + 1)

        for j in range(QT + S_LAG):
            if j < QT:
                e_tiles[j] = e_pool.tile([P, K], F32, tag="e", name="e")
                if SPLIT and j == 0:
                    q_exp(0, 0, NH, s_half[:, 0:1])
                    q_exp(0, NH, K, s_half[:, 1:2])
                else:
                    q_exp(j, 0, K, s_all[:, j:j + 1])
            if j - S_LAG >= 0 and j - S_LAG in NORM_ON_SCALAR:
                q_norm(j - S_LAG)
            if j < QT:
                if SPLIT and j == 0:
                    q_entropy_sum(0, 0, NH, ed_half[:, 0:1])
                    q_entropy_sum(0, NH, K, ed_half[:, 1:2])
                    nc.vector.tensor_tensor(out=s_first[:], in0=s_half[:, 0:1], in1=s_half[:, 1:2],
                                            op=ALU.add)
                    nc.vector.tensor_tensor(out=ed_all[:, 0:1], in0=ed_half[:, 0:1],
                                            in1=ed_half[:, 1:2], op=ALU.add)
                    nc.vector.reciprocal(out=c_all[:, 0:1], in_=s_first[:])
                    q_norm(0)
                elif j == LAST:
                    nc.vector.reciprocal(out=c_all[:, j:j + 1], in_=s_all[:, j:j + 1])
                    nc.scalar.activation(out=ln_c[:], in_=c_all[:], func=ACT.Ln)
                    q_norm(j)
                    q_entropy_sum(j, 0, K, ed_all[:, j:j + 1])
                else:
                    nc.vector.reciprocal(out=c_all[:, j:j + 1], in_=s_all[:, j:j + 1])
                    q_entropy_sum(j, 0, K, ed_all[:, j:j + 1])
                    if j not in NORM_ON_SCALAR:
                        q_norm(j)

        nc.sync.dma_start(out=out_1.rearrange("(p j) -> p j", j=QT), in_=c_all[:])
        nc.vector.tensor_tensor(out=h_tmp[:], in0=ed_all[:], in1=c_all[:], op=ALU.mult)
        nc.vector.tensor_tensor(out=h_all[:], in0=h_tmp[:], in1=ln_c[:], op=ALU.subtract)
        nc.sync.dma_start(out=out_2.rearrange("(p j) -> p j", j=QT), in_=h_all[:])
